import numpy as np
import ml_dtypes

BF16 = ml_dtypes.bfloat16


def bf(x):
    return np.asarray(x, np.float32).astype(BF16)


def f32(x):
    return np.asarray(x, np.float32)


def f64(x):
    return np.asarray(x).astype(np.float64)


def striped(idx):
    return np.tile(idx.reshape(-1, 16).T, (8, 1))


C, S, N, NH, NL, O, GS = 1024, 1024, 512, 128, 384, 512, 128
HALF_HI, HALF_LO = 31, 15
LV_HI, LV_LO = 64, 32


def dequant(q, scales, half):
    return (f64(q) - half) * np.repeat(f64(scales), GS, axis=0)


def setup_inputs():
    return {"x": f32(np.random.standard_normal((C, S))), "q_high": bf(np.random.choice(LV_HI, size=(NH, O))), "q_low": bf(np.random.choice(LV_LO, size=(NL, O))), "scales_high": f32(np.random.random((NH // GS, O)) * 0.02 + 1e-4), "scales_low": f32(np.random.random((NL // GS, O)) * 0.02 + 1e-4), "bias": f32(0.3 * np.random.standard_normal((1, O))), "offs": striped(np.random.permutation(S)[:N])}


def reference(x, q_high, q_low, scales_high, scales_low, bias, offs):
    idx = offs[:16].T.reshape(-1)
    xp = f64(x)[:, idx]
    w_high = dequant(q_high, scales_high, HALF_HI)
    w_low = dequant(q_low, scales_low, HALF_LO)
    return xp[:, :NH] @ w_high + xp[:, NH:] @ w_low + f64(bias)

@@ -1,0 +1,80 @@
+import concourse.mybir as mybir
+from concourse.masks import make_identity
+
+F32, BF16, U16 = mybir.dt.float32, mybir.dt.bfloat16, mybir.dt.uint16
+COPY = mybir.ActivationFunctionType.Copy
+ADD, SUBTRACT, MULT = mybir.AluOpType.add, mybir.AluOpType.subtract, mybir.AluOpType.mult
+
+P = 128
+TOKENS = 1024
+FEATURES = 1024
+PICKED = 512
+OUT = 512
+GROUP = 128
+N_GROUPS = PICKED // GROUP
+N_BLOCKS = TOKENS // P
+HALF_HIGH, HALF_LOW = 31.0, 15.0
+
+FLOPS = 2 * TOKENS * PICKED * OUT
+
+
+def tile_cprpackedlinear_kernel(tc, x, q_high, q_low, scales_high, scales_low, bias, offs, out):
+    nc = tc.nc
+    with (
+        tc.tile_pool(name="held", bufs=1) as held,
+        tc.tile_pool(name="work", bufs=3) as work,
+        tc.psum_pool(name="flip_banks", bufs=2) as flip_banks,
+        tc.psum_pool(name="sum_banks", bufs=2) as sum_banks,
+    ):
+        offsets = held.tile([P, PICKED // 16], U16, name="offsets")
+        nc.sync.dma_start(offsets[:], offs)
+        windows = []
+        for b in range(N_BLOCKS):
+            window = held.tile([P, FEATURES], F32, name=f"window{b}")
+            nc.sync.dma_start(window[:], x[b * P : (b + 1) * P, :])
+            windows.append(window)
+
+        identity = held.tile([P, P], F32, name="identity")
+        make_identity(nc, identity[:])
+
+        weights = []
+        for g in range(N_GROUPS):
+            codes = held.tile([P, OUT], BF16, name=f"codes{g}")
+            scales = held.tile([P, OUT], F32, name=f"scales{g}")
+            if g == 0:
+                nc.scalar.dma_start(codes[:], q_high)
+                nc.scalar.dma_start(scales[:], scales_high[0, :].partition_broadcast(P))
+            else:
+                nc.scalar.dma_start(codes[:], q_low[(g - 1) * GROUP : g * GROUP, :])
+                nc.scalar.dma_start(scales[:], scales_low[g - 1, :].partition_broadcast(P))
+            weight = held.tile([P, OUT], BF16, name=f"weight{g}")
+            nc.vector.scalar_tensor_tensor(
+                weight[:], codes[:], HALF_HIGH if g == 0 else HALF_LOW, scales[:], SUBTRACT, MULT
+            )
+            weights.append(weight)
+        bias_rows = held.tile([P, OUT], F32, name="bias_rows")
+        nc.scalar.dma_start(bias_rows[:], bias[0, :].partition_broadcast(P))
+
+        for b in range(N_BLOCKS):
+            picked = work.tile([P, PICKED], F32, name="picked")
+            nc.scalar.activation(picked[:], windows[b][:].indirect(offsets[:]), COPY)
+
+            flipped_f32 = flip_banks.tile([P, PICKED], F32, name="flipped_f32")
+            for g in range(N_GROUPS):
+                square = slice(g * GROUP, (g + 1) * GROUP)
+                nc.tensor.transpose(flipped_f32[:, square], picked[:, square], identity[:])
+            flipped = work.tile([P, PICKED], BF16, name="flipped")
+            nc.vector.tensor_copy(flipped[:], flipped_f32[:])
+
+            sums = sum_banks.tile([P, OUT], F32, name="sums")
+            for g in range(N_GROUPS):
+                nc.tensor.matmul(
+                    sums[:],
+                    flipped[:, g * GROUP : (g + 1) * GROUP],
+                    weights[g][:],
+                    start=(g == 0),
+                    stop=(g == N_GROUPS - 1),
+                )
+            result = work.tile([P, OUT], F32, name="result")
+            nc.vector.tensor_tensor(result[:], sums[:], bias_rows[:], ADD)
+            nc.sync.dma_start(out[b * P : (b + 1) * P, :], result[:])

@@ -17,24 +17,30 @@ HALF_HIGH, HALF_LOW = 31.0, 15.0
 
 FLOPS = 2 * TOKENS * PICKED * OUT
 
+BLOCKS_BEFORE_WEIGHTS = 2
+
 
 def tile_cprpackedlinear_kernel(tc, x, q_high, q_low, scales_high, scales_low, bias, offs, out):
     nc = tc.nc
     with (
         tc.tile_pool(name="held", bufs=1) as held,
         tc.tile_pool(name="work", bufs=3) as work,
+        tc.tile_pool(name="results", bufs=N_BLOCKS) as results,
         tc.psum_pool(name="flip_banks", bufs=2) as flip_banks,
         tc.psum_pool(name="sum_banks", bufs=2) as sum_banks,
     ):
         offsets = held.tile([P, PICKED // 16], U16, name="offsets")
         nc.sync.dma_start(offsets[:], offs)
-        windows = []
-        for b in range(N_BLOCKS):
-            window = held.tile([P, FEATURES], F32, name=f"window{b}")
-            nc.sync.dma_start(window[:], x[b * P : (b + 1) * P, :])
-            windows.append(window)
 
-        identity = held.tile([P, P], F32, name="identity")
+        windows = [held.tile([P, FEATURES], F32, name=f"window{b}") for b in range(N_BLOCKS)]
+        for b in range(BLOCKS_BEFORE_WEIGHTS):
+            nc.sync.dma_start(windows[b][:], x[b * P : (b + 1) * P, :])
+
+        warm = held.tile([P, 2], F32, name="warm")
+        nc.vector.memset(warm[:, 0:1], 0.0)
+        nc.scalar.activation(warm[:, 1:2], warm[:, 0:1], COPY)
+
+        identity = held.tile([P, P], BF16, name="identity")
         make_identity(nc, identity[:])
 
         weights = []
@@ -42,30 +48,36 @@ def tile_cprpackedlinear_kernel(tc, x, q_high, q_low, scales_high, scales_low, b
             codes = held.tile([P, OUT], BF16, name=f"codes{g}")
             scales = held.tile([P, OUT], F32, name=f"scales{g}")
             if g == 0:
-                nc.scalar.dma_start(codes[:], q_high)
-                nc.scalar.dma_start(scales[:], scales_high[0, :].partition_broadcast(P))
+                nc.sync.dma_start(codes[:], q_high)
+                nc.sync.dma_start(scales[:], scales_high[0, :].partition_broadcast(P))
             else:
-                nc.scalar.dma_start(codes[:], q_low[(g - 1) * GROUP : g * GROUP, :])
-                nc.scalar.dma_start(scales[:], scales_low[g - 1, :].partition_broadcast(P))
+                nc.sync.dma_start(codes[:], q_low[(g - 1) * GROUP : g * GROUP, :])
+                nc.sync.dma_start(scales[:], scales_low[g - 1, :].partition_broadcast(P))
             weight = held.tile([P, OUT], BF16, name=f"weight{g}")
             nc.vector.scalar_tensor_tensor(
                 weight[:], codes[:], HALF_HIGH if g == 0 else HALF_LOW, scales[:], SUBTRACT, MULT
             )
             weights.append(weight)
         bias_rows = held.tile([P, OUT], F32, name="bias_rows")
-        nc.scalar.dma_start(bias_rows[:], bias[0, :].partition_broadcast(P))
+        nc.sync.dma_start(bias_rows[:], bias[0, :].partition_broadcast(P))
 
-        for b in range(N_BLOCKS):
+        for b in range(BLOCKS_BEFORE_WEIGHTS, N_BLOCKS):
+            nc.sync.dma_start(windows[b][:], x[b * P : (b + 1) * P, :])
+
+        def look_up_and_flip(b):
             picked = work.tile([P, PICKED], F32, name="picked")
             nc.scalar.activation(picked[:], windows[b][:].indirect(offsets[:]), COPY)
-
-            flipped_f32 = flip_banks.tile([P, PICKED], F32, name="flipped_f32")
+            rounded = work.tile([P, PICKED], BF16, name="rounded")
+            nc.gpsimd.tensor_copy(rounded[:], picked[:])
+            flipped_psum = flip_banks.tile([P, PICKED], BF16, name="flipped_psum")
             for g in range(N_GROUPS):
                 square = slice(g * GROUP, (g + 1) * GROUP)
-                nc.tensor.transpose(flipped_f32[:, square], picked[:, square], identity[:])
+                nc.tensor.transpose(flipped_psum[:, square], rounded[:, square], identity[:])
             flipped = work.tile([P, PICKED], BF16, name="flipped")
-            nc.vector.tensor_copy(flipped[:], flipped_f32[:])
+            nc.vector.tensor_copy(flipped[:], flipped_psum[:])
+            return flipped
 
+        def multiply_and_store(b, flipped):
             sums = sum_banks.tile([P, OUT], F32, name="sums")
             for g in range(N_GROUPS):
                 nc.tensor.matmul(
@@ -75,6 +87,12 @@ def tile_cprpackedlinear_kernel(tc, x, q_high, q_low, scales_high, scales_low, b
                     start=(g == 0),
                     stop=(g == N_GROUPS - 1),
                 )
-            result = work.tile([P, OUT], F32, name="result")
+            result = results.tile([P, OUT], F32, name="result")
             nc.vector.tensor_tensor(result[:], sums[:], bias_rows[:], ADD)
             nc.sync.dma_start(out[b * P : (b + 1) * P, :], result[:])
+
+        flipped_now = look_up_and_flip(0)
+        for b in range(N_BLOCKS):
+            flipped_next = look_up_and_flip(b + 1) if b + 1 < N_BLOCKS else None
+            multiply_and_store(b, flipped_now)
+            flipped_now = flipped_next

@@ -17,6 +17,7 @@ HALF_HIGH, HALF_LOW = 31.0, 15.0
 
 FLOPS = 2 * TOKENS * PICKED * OUT
 
+N_WARM = 12
 BLOCKS_BEFORE_WEIGHTS = 2
 
 
@@ -42,6 +43,12 @@ def tile_cprpackedlinear_kernel(tc, x, q_high, q_low, scales_high, scales_low, b
 
         identity = held.tile([P, P], BF16, name="identity")
         make_identity(nc, identity[:])
+
+        zeros = held.tile([P, OUT], BF16, name="zeros")
+        nc.vector.memset(zeros[:], 0.0)
+        unread = sum_banks.tile([P, OUT], F32, name="unread")
+        for i in range(N_WARM):
+            nc.tensor.matmul(unread[:], identity[:], zeros[:], start=True, stop=True)
 
         weights = []
         for g in range(N_GROUPS):

@@ -17,7 +17,6 @@ HALF_HIGH, HALF_LOW = 31.0, 15.0
 
 FLOPS = 2 * TOKENS * PICKED * OUT
 
-N_WARM = 12
 BLOCKS_BEFORE_WEIGHTS = 2
 
 
@@ -25,10 +24,10 @@ def tile_cprpackedlinear_kernel(tc, x, q_high, q_low, scales_high, scales_low, b
     nc = tc.nc
     with (
         tc.tile_pool(name="held", bufs=1) as held,
-        tc.tile_pool(name="work", bufs=3) as work,
+        tc.tile_pool(name="work", bufs=4) as work,
         tc.tile_pool(name="results", bufs=N_BLOCKS) as results,
-        tc.psum_pool(name="flip_banks", bufs=2) as flip_banks,
-        tc.psum_pool(name="sum_banks", bufs=2) as sum_banks,
+        tc.psum_pool(name="flip_banks", bufs=3) as flip_banks,
+        tc.psum_pool(name="sum_banks", bufs=3) as sum_banks,
     ):
         offsets = held.tile([P, PICKED // 16], U16, name="offsets")
         nc.sync.dma_start(offsets[:], offs)
@@ -37,39 +36,35 @@ def tile_cprpackedlinear_kernel(tc, x, q_high, q_low, scales_high, scales_low, b
         for b in range(BLOCKS_BEFORE_WEIGHTS):
             nc.sync.dma_start(windows[b][:], x[b * P : (b + 1) * P, :])
 
-        warm = held.tile([P, 2], F32, name="warm")
-        nc.vector.memset(warm[:, 0:1], 0.0)
-        nc.scalar.activation(warm[:, 1:2], warm[:, 0:1], COPY)
-
-        identity = held.tile([P, P], BF16, name="identity")
-        make_identity(nc, identity[:])
-
-        zeros = held.tile([P, OUT], BF16, name="zeros")
-        nc.vector.memset(zeros[:], 0.0)
-        unread = sum_banks.tile([P, OUT], F32, name="unread")
-        for i in range(N_WARM):
-            nc.tensor.matmul(unread[:], identity[:], zeros[:], start=True, stop=True)
-
-        weights = []
-        for g in range(N_GROUPS):
-            codes = held.tile([P, OUT], BF16, name=f"codes{g}")
-            scales = held.tile([P, OUT], F32, name=f"scales{g}")
-            if g == 0:
-                nc.sync.dma_start(codes[:], q_high)
-                nc.sync.dma_start(scales[:], scales_high[0, :].partition_broadcast(P))
-            else:
-                nc.sync.dma_start(codes[:], q_low[(g - 1) * GROUP : g * GROUP, :])
-                nc.sync.dma_start(scales[:], scales_low[g - 1, :].partition_broadcast(P))
-            weight = held.tile([P, OUT], BF16, name=f"weight{g}")
-            nc.vector.scalar_tensor_tensor(
-                weight[:], codes[:], HALF_HIGH if g == 0 else HALF_LOW, scales[:], SUBTRACT, MULT
-            )
-            weights.append(weight)
+        codes = held.tile([P, N_GROUPS * OUT], BF16, name="codes")
+        scales = held.tile([P, N_GROUPS * OUT], F32, name="scales")
         bias_rows = held.tile([P, OUT], F32, name="bias_rows")
+        nc.sync.dma_start(codes[:, 0:OUT], q_high)
+        nc.sync.dma_start(scales[:, 0:OUT], scales_high[0, :].partition_broadcast(P))
+        nc.sync.dma_start(
+            codes[:, OUT:].rearrange("p (g o) -> p g o", o=OUT), q_low.rearrange("(g p) o -> p g o", p=P)
+        )
+        nc.sync.dma_start(scales[:, OUT:], scales_low.rearrange("g o -> (g o)").partition_broadcast(P))
         nc.sync.dma_start(bias_rows[:], bias[0, :].partition_broadcast(P))
 
         for b in range(BLOCKS_BEFORE_WEIGHTS, N_BLOCKS):
             nc.sync.dma_start(windows[b][:], x[b * P : (b + 1) * P, :])
+
+        warm_in = held.tile([P, 1], F32, name="warm_in")
+        warm_out = held.tile([P, 1], F32, name="warm_out")
+        nc.vector.memset(warm_in[:], 0.0)
+        nc.scalar.activation(warm_out[:], warm_in[:], COPY)
+
+        identity = held.tile([P, P], BF16, name="identity")
+        make_identity(nc, identity[:])
+
+        weights = held.tile([P, N_GROUPS * OUT], BF16, name="weights")
+        for g in range(N_GROUPS):
+            columns = slice(g * OUT, (g + 1) * OUT)
+            nc.vector.scalar_tensor_tensor(
+                weights[:, columns], codes[:, columns], HALF_HIGH if g == 0 else HALF_LOW, scales[:, columns],
+                SUBTRACT, MULT,
+            )
 
         def look_up_and_flip(b):
             picked = work.tile([P, PICKED], F32, name="picked")
@@ -90,7 +85,7 @@ def tile_cprpackedlinear_kernel(tc, x, q_high, q_low, scales_high, scales_low, b
                 nc.tensor.matmul(
                     sums[:],
                     flipped[:, g * GROUP : (g + 1) * GROUP],
-                    weights[g][:],
+                    weights[:, g * OUT : (g + 1) * OUT],
                     start=(g == 0),
                     stop=(g == N_GROUPS - 1),
                 )
@@ -98,8 +93,8 @@ def tile_cprpackedlinear_kernel(tc, x, q_high, q_low, scales_high, scales_low, b
             nc.vector.tensor_tensor(result[:], sums[:], bias_rows[:], ADD)
             nc.sync.dma_start(out[b * P : (b + 1) * P, :], result[:])
 
-        flipped_now = look_up_and_flip(0)
+        flipped_tiles = [look_up_and_flip(0)]
         for b in range(N_BLOCKS):
-            flipped_next = look_up_and_flip(b + 1) if b + 1 < N_BLOCKS else None
-            multiply_and_store(b, flipped_now)
-            flipped_now = flipped_next
+            if b + 1 < N_BLOCKS:
+                flipped_tiles.append(look_up_and_flip(b + 1))
+            multiply_and_store(b, flipped_tiles[b])

@@ -17,6 +17,9 @@ HALF_HIGH, HALF_LOW = 31.0, 15.0
 
 FLOPS = 2 * TOKENS * PICKED * OUT
 
+PIECE = 256
+GROUPS_IN_PIECE = PIECE // GROUP
+N_PIECES = PICKED // PIECE
 BLOCKS_BEFORE_WEIGHTS = 2
 
 
@@ -24,9 +27,9 @@ def tile_cprpackedlinear_kernel(tc, x, q_high, q_low, scales_high, scales_low, b
     nc = tc.nc
     with (
         tc.tile_pool(name="held", bufs=1) as held,
-        tc.tile_pool(name="work", bufs=4) as work,
+        tc.tile_pool(name="work", bufs=6) as work,
         tc.tile_pool(name="results", bufs=N_BLOCKS) as results,
-        tc.psum_pool(name="flip_banks", bufs=3) as flip_banks,
+        tc.psum_pool(name="flip_banks", bufs=4) as flip_banks,
         tc.psum_pool(name="sum_banks", bufs=3) as sum_banks,
     ):
         offsets = held.tile([P, PICKED // 16], U16, name="offsets")
@@ -66,35 +69,41 @@ def tile_cprpackedlinear_kernel(tc, x, q_high, q_low, scales_high, scales_low, b
                 SUBTRACT, MULT,
             )
 
-        def look_up_and_flip(b):
-            picked = work.tile([P, PICKED], F32, name="picked")
-            nc.scalar.activation(picked[:], windows[b][:].indirect(offsets[:]), COPY)
-            rounded = work.tile([P, PICKED], BF16, name="rounded")
+        def look_up_and_flip(b, i):
+            picked = work.tile([P, PIECE], F32, name="picked")
+            nc.scalar.activation(
+                picked[:], windows[b][:].indirect(offsets[:, i * PIECE // 16 : (i + 1) * PIECE // 16]), COPY
+            )
+            rounded = work.tile([P, PIECE], BF16, name="rounded")
             nc.gpsimd.tensor_copy(rounded[:], picked[:])
-            flipped_psum = flip_banks.tile([P, PICKED], BF16, name="flipped_psum")
-            for g in range(N_GROUPS):
-                square = slice(g * GROUP, (g + 1) * GROUP)
+            flipped_psum = flip_banks.tile([P, PIECE], BF16, name="flipped_psum")
+            for k in range(GROUPS_IN_PIECE):
+                square = slice(k * GROUP, (k + 1) * GROUP)
                 nc.tensor.transpose(flipped_psum[:, square], rounded[:, square], identity[:])
-            flipped = work.tile([P, PICKED], BF16, name="flipped")
+            flipped = work.tile([P, PIECE], BF16, name="flipped")
             nc.vector.tensor_copy(flipped[:], flipped_psum[:])
             return flipped
 
-        def multiply_and_store(b, flipped):
-            sums = sum_banks.tile([P, OUT], F32, name="sums")
-            for g in range(N_GROUPS):
+        def multiply(sums, i, flipped):
+            for k in range(GROUPS_IN_PIECE):
+                g = i * GROUPS_IN_PIECE + k
                 nc.tensor.matmul(
                     sums[:],
-                    flipped[:, g * GROUP : (g + 1) * GROUP],
+                    flipped[:, k * GROUP : (k + 1) * GROUP],
                     weights[:, g * OUT : (g + 1) * OUT],
                     start=(g == 0),
                     stop=(g == N_GROUPS - 1),
                 )
-            result = results.tile([P, OUT], F32, name="result")
-            nc.vector.tensor_tensor(result[:], sums[:], bias_rows[:], ADD)
-            nc.sync.dma_start(out[b * P : (b + 1) * P, :], result[:])
 
-        flipped_tiles = [look_up_and_flip(0)]
-        for b in range(N_BLOCKS):
-            if b + 1 < N_BLOCKS:
-                flipped_tiles.append(look_up_and_flip(b + 1))
-            multiply_and_store(b, flipped_tiles[b])
+        steps = [(b, i) for b in range(N_BLOCKS) for i in range(N_PIECES)]
+        flipped_tiles = [look_up_and_flip(0, 0)]
+        for s, (b, i) in enumerate(steps):
+            if s + 1 < len(steps):
+                flipped_tiles.append(look_up_and_flip(*steps[s + 1]))
+            if i == 0:
+                sums = sum_banks.tile([P, OUT], F32, name="sums")
+            multiply(sums, i, flipped_tiles[s])
+            if i == N_PIECES - 1:
+                result = results.tile([P, OUT], F32, name="result")
+                nc.vector.tensor_tensor(result[:], sums[:], bias_rows[:], ADD)
+                nc.sync.dma_start(out[b * P : (b + 1) * P, :], result[:])

@@ -17,19 +17,16 @@ HALF_HIGH, HALF_LOW = 31.0, 15.0
 
 FLOPS = 2 * TOKENS * PICKED * OUT
 
-PIECE = 256
-GROUPS_IN_PIECE = PIECE // GROUP
-N_PIECES = PICKED // PIECE
-BLOCKS_BEFORE_WEIGHTS = 2
+BLOCKS_BEFORE_WEIGHTS = 1
 
 
 def tile_cprpackedlinear_kernel(tc, x, q_high, q_low, scales_high, scales_low, bias, offs, out):
     nc = tc.nc
     with (
         tc.tile_pool(name="held", bufs=1) as held,
-        tc.tile_pool(name="work", bufs=6) as work,
+        tc.tile_pool(name="work", bufs=4) as work,
         tc.tile_pool(name="results", bufs=N_BLOCKS) as results,
-        tc.psum_pool(name="flip_banks", bufs=4) as flip_banks,
+        tc.psum_pool(name="flip_banks", bufs=3) as flip_banks,
         tc.psum_pool(name="sum_banks", bufs=3) as sum_banks,
     ):
         offsets = held.tile([P, PICKED // 16], U16, name="offsets")
@@ -69,41 +66,35 @@ def tile_cprpackedlinear_kernel(tc, x, q_high, q_low, scales_high, scales_low, b
                 SUBTRACT, MULT,
             )
 
-        def look_up_and_flip(b, i):
-            picked = work.tile([P, PIECE], F32, name="picked")
-            nc.scalar.activation(
-                picked[:], windows[b][:].indirect(offsets[:, i * PIECE // 16 : (i + 1) * PIECE // 16]), COPY
-            )
-            rounded = work.tile([P, PIECE], BF16, name="rounded")
+        def look_up_and_flip(b):
+            picked = work.tile([P, PICKED], F32, name="picked")
+            nc.scalar.activation(picked[:], windows[b][:].indirect(offsets[:]), COPY)
+            rounded = work.tile([P, PICKED], BF16, name="rounded")
             nc.gpsimd.tensor_copy(rounded[:], picked[:])
-            flipped_psum = flip_banks.tile([P, PIECE], BF16, name="flipped_psum")
-            for k in range(GROUPS_IN_PIECE):
-                square = slice(k * GROUP, (k + 1) * GROUP)
+            flipped_psum = flip_banks.tile([P, PICKED], BF16, name="flipped_psum")
+            for g in range(N_GROUPS):
+                square = slice(g * GROUP, (g + 1) * GROUP)
                 nc.tensor.transpose(flipped_psum[:, square], rounded[:, square], identity[:])
-            flipped = work.tile([P, PIECE], BF16, name="flipped")
+            flipped = work.tile([P, PICKED], BF16, name="flipped")
             nc.vector.tensor_copy(flipped[:], flipped_psum[:])
             return flipped
 
-        def multiply(sums, i, flipped):
-            for k in range(GROUPS_IN_PIECE):
-                g = i * GROUPS_IN_PIECE + k
+        def multiply_and_store(b, flipped):
+            sums = sum_banks.tile([P, OUT], F32, name="sums")
+            for g in range(N_GROUPS):
                 nc.tensor.matmul(
                     sums[:],
-                    flipped[:, k * GROUP : (k + 1) * GROUP],
+                    flipped[:, g * GROUP : (g + 1) * GROUP],
                     weights[:, g * OUT : (g + 1) * OUT],
                     start=(g == 0),
                     stop=(g == N_GROUPS - 1),
                 )
+            result = results.tile([P, OUT], F32, name="result")
+            nc.vector.tensor_tensor(result[:], sums[:], bias_rows[:], ADD)
+            nc.sync.dma_start(out[b * P : (b + 1) * P, :], result[:])
 
-        steps = [(b, i) for b in range(N_BLOCKS) for i in range(N_PIECES)]
-        flipped_tiles = [look_up_and_flip(0, 0)]
-        for s, (b, i) in enumerate(steps):
-            if s + 1 < len(steps):
-                flipped_tiles.append(look_up_and_flip(*steps[s + 1]))
-            if i == 0:
-                sums = sum_banks.tile([P, OUT], F32, name="sums")
-            multiply(sums, i, flipped_tiles[s])
-            if i == N_PIECES - 1:
-                result = results.tile([P, OUT], F32, name="result")
-                nc.vector.tensor_tensor(result[:], sums[:], bias_rows[:], ADD)
-                nc.sync.dma_start(out[b * P : (b + 1) * P, :], result[:])
+        flipped_tiles = [look_up_and_flip(0)]
+        for b in range(N_BLOCKS):
+            if b + 1 < N_BLOCKS:
+                flipped_tiles.append(look_up_and_flip(b + 1))
+            multiply_and_store(b, flipped_tiles[b])

@@ -17,7 +17,7 @@ HALF_HIGH, HALF_LOW = 31.0, 15.0
 
 FLOPS = 2 * TOKENS * PICKED * OUT
 
-BLOCKS_BEFORE_WEIGHTS = 1
+BLOCKS_BEFORE_WEIGHTS = 2
 
 
 def tile_cprpackedlinear_kernel(tc, x, q_high, q_low, scales_high, scales_low, bias, offs, out):
@@ -26,26 +26,29 @@ def tile_cprpackedlinear_kernel(tc, x, q_high, q_low, scales_high, scales_low, b
         tc.tile_pool(name="held", bufs=1) as held,
         tc.tile_pool(name="work", bufs=4) as work,
         tc.tile_pool(name="results", bufs=N_BLOCKS) as results,
+        tc.psum_pool(name="row_banks", bufs=1) as row_banks,
         tc.psum_pool(name="flip_banks", bufs=3) as flip_banks,
         tc.psum_pool(name="sum_banks", bufs=3) as sum_banks,
     ):
         offsets = held.tile([P, PICKED // 16], U16, name="offsets")
         nc.sync.dma_start(offsets[:], offs)
 
+        scales_high_row = held.tile([1, OUT], F32, name="scales_high_row")
+        bias_row = held.tile([1, OUT], F32, name="bias_row")
+        nc.sync.dma_start(scales_high_row[:], scales_high)
+        nc.sync.dma_start(bias_row[:], bias)
+
         windows = [held.tile([P, FEATURES], F32, name=f"window{b}") for b in range(N_BLOCKS)]
         for b in range(BLOCKS_BEFORE_WEIGHTS):
             nc.sync.dma_start(windows[b][:], x[b * P : (b + 1) * P, :])
 
         codes = held.tile([P, N_GROUPS * OUT], BF16, name="codes")
-        scales = held.tile([P, N_GROUPS * OUT], F32, name="scales")
-        bias_rows = held.tile([P, OUT], F32, name="bias_rows")
+        scales_low_rows = held.tile([P, (N_GROUPS - 1) * OUT], F32, name="scales_low_rows")
         nc.sync.dma_start(codes[:, 0:OUT], q_high)
-        nc.sync.dma_start(scales[:, 0:OUT], scales_high[0, :].partition_broadcast(P))
         nc.sync.dma_start(
             codes[:, OUT:].rearrange("p (g o) -> p g o", o=OUT), q_low.rearrange("(g p) o -> p g o", p=P)
         )
-        nc.sync.dma_start(scales[:, OUT:], scales_low.rearrange("g o -> (g o)").partition_broadcast(P))
-        nc.sync.dma_start(bias_rows[:], bias[0, :].partition_broadcast(P))
+        nc.sync.dma_start(scales_low_rows[:], scales_low.rearrange("g o -> (g o)").partition_broadcast(P))
 
         for b in range(BLOCKS_BEFORE_WEIGHTS, N_BLOCKS):
             nc.sync.dma_start(windows[b][:], x[b * P : (b + 1) * P, :])
@@ -58,12 +61,27 @@ def tile_cprpackedlinear_kernel(tc, x, q_high, q_low, scales_high, scales_low, b
         identity = held.tile([P, P], BF16, name="identity")
         make_identity(nc, identity[:])
 
+        ones = held.tile([1, P], F32, name="ones")
+        nc.vector.memset(ones[:], 1.0)
+        scales_high_rows = row_banks.tile([P, OUT], F32, name="scales_high_rows")
+        nc.tensor.matmul(scales_high_rows[:], ones[:], scales_high_row[:], start=True, stop=True)
+        bias_bank = row_banks.tile([P, OUT], F32, name="bias_bank")
+        nc.tensor.matmul(bias_bank[:], ones[:], bias_row[:], start=True, stop=True)
+        bias_rows = held.tile([P, OUT], F32, name="bias_rows")
+        nc.vector.tensor_copy(bias_rows[:], bias_bank[:])
+
         weights = held.tile([P, N_GROUPS * OUT], BF16, name="weights")
-        for g in range(N_GROUPS):
-            columns = slice(g * OUT, (g + 1) * OUT)
+        nc.vector.scalar_tensor_tensor(
+            weights[:, 0:OUT], codes[:, 0:OUT], HALF_HIGH, scales_high_rows[:], SUBTRACT, MULT
+        )
+        for g in range(1, N_GROUPS):
             nc.vector.scalar_tensor_tensor(
-                weights[:, columns], codes[:, columns], HALF_HIGH if g == 0 else HALF_LOW, scales[:, columns],
-                SUBTRACT, MULT,
+                weights[:, g * OUT : (g + 1) * OUT],
+                codes[:, g * OUT : (g + 1) * OUT],
+                HALF_LOW,
+                scales_low_rows[:, (g - 1) * OUT : g * OUT],
+                SUBTRACT,
+                MULT,
             )
 
         def look_up_and_flip(b):

@@ -17,6 +17,9 @@ HALF_HIGH, HALF_LOW = 31.0, 15.0
 
 FLOPS = 2 * TOKENS * PICKED * OUT
 
+N_ROWS = N_GROUPS + 1
+PIECES = OUT // P
+BLOCKS_AHEAD = 2
 BLOCKS_BEFORE_WEIGHTS = 2
 
 
@@ -26,29 +29,27 @@ def tile_cprpackedlinear_kernel(tc, x, q_high, q_low, scales_high, scales_low, b
         tc.tile_pool(name="held", bufs=1) as held,
         tc.tile_pool(name="work", bufs=4) as work,
         tc.tile_pool(name="results", bufs=N_BLOCKS) as results,
-        tc.psum_pool(name="row_banks", bufs=1) as row_banks,
         tc.psum_pool(name="flip_banks", bufs=3) as flip_banks,
-        tc.psum_pool(name="sum_banks", bufs=3) as sum_banks,
+        tc.psum_pool(name="float_banks", bufs=N_ROWS) as float_banks,
     ):
         offsets = held.tile([P, PICKED // 16], U16, name="offsets")
         nc.sync.dma_start(offsets[:], offs)
 
-        scales_high_row = held.tile([1, OUT], F32, name="scales_high_row")
-        bias_row = held.tile([1, OUT], F32, name="bias_row")
-        nc.sync.dma_start(scales_high_row[:], scales_high)
-        nc.sync.dma_start(bias_row[:], bias)
+        row_pieces = held.tile([P, P], F32, name="row_pieces")
+        nc.gpsimd.memset(row_pieces[:], 0.0)
+        nc.sync.dma_start(row_pieces[0:PIECES, :], scales_high.rearrange("g (k n) -> (g k) n", n=P))
+        nc.sync.dma_start(row_pieces[PIECES : N_GROUPS * PIECES, :], scales_low.rearrange("g (k n) -> (g k) n", n=P))
+        nc.sync.dma_start(row_pieces[N_GROUPS * PIECES : N_ROWS * PIECES, :], bias.rearrange("g (k n) -> (g k) n", n=P))
 
         windows = [held.tile([P, FEATURES], F32, name=f"window{b}") for b in range(N_BLOCKS)]
         for b in range(BLOCKS_BEFORE_WEIGHTS):
             nc.sync.dma_start(windows[b][:], x[b * P : (b + 1) * P, :])
 
         codes = held.tile([P, N_GROUPS * OUT], BF16, name="codes")
-        scales_low_rows = held.tile([P, (N_GROUPS - 1) * OUT], F32, name="scales_low_rows")
         nc.sync.dma_start(codes[:, 0:OUT], q_high)
         nc.sync.dma_start(
             codes[:, OUT:].rearrange("p (g o) -> p g o", o=OUT), q_low.rearrange("(g p) o -> p g o", p=P)
         )
-        nc.sync.dma_start(scales_low_rows[:], scales_low.rearrange("g o -> (g o)").partition_broadcast(P))
 
         for b in range(BLOCKS_BEFORE_WEIGHTS, N_BLOCKS):
             nc.sync.dma_start(windows[b][:], x[b * P : (b + 1) * P, :])
@@ -60,29 +61,30 @@ def tile_cprpackedlinear_kernel(tc, x, q_high, q_low, scales_high, scales_low, b
 
         identity = held.tile([P, P], BF16, name="identity")
         make_identity(nc, identity[:])
+        identity_f32 = held.tile([P, P], F32, name="identity_f32")
+        make_identity(nc, identity_f32[:])
 
-        ones = held.tile([1, P], F32, name="ones")
-        nc.vector.memset(ones[:], 1.0)
-        scales_high_rows = row_banks.tile([P, OUT], F32, name="scales_high_rows")
-        nc.tensor.matmul(scales_high_rows[:], ones[:], scales_high_row[:], start=True, stop=True)
-        bias_bank = row_banks.tile([P, OUT], F32, name="bias_bank")
-        nc.tensor.matmul(bias_bank[:], ones[:], bias_row[:], start=True, stop=True)
-        bias_rows = held.tile([P, OUT], F32, name="bias_rows")
-        nc.vector.tensor_copy(bias_rows[:], bias_bank[:])
+        columns_bank = float_banks.tile([P, P], F32, name="columns_bank", tag="float_bank")
+        nc.tensor.transpose(columns_bank[:], row_pieces[:], identity_f32[:])
+        columns = held.tile([P, N_ROWS * PIECES], F32, name="columns")
+        nc.vector.tensor_copy(columns[:], columns_bank[:, 0 : N_ROWS * PIECES])
+
+        def repeat_on_all_partitions(r):
+            repeated = float_banks.tile([P, OUT], F32, name="repeated", tag="float_bank")
+            for k in range(PIECES):
+                column = columns[:, r * PIECES + k : r * PIECES + k + 1]
+                nc.tensor.transpose(repeated[:, k * P : (k + 1) * P], column.to_broadcast([P, P]), identity_f32[:])
+            return repeated
 
         weights = held.tile([P, N_GROUPS * OUT], BF16, name="weights")
-        nc.vector.scalar_tensor_tensor(
-            weights[:, 0:OUT], codes[:, 0:OUT], HALF_HIGH, scales_high_rows[:], SUBTRACT, MULT
-        )
-        for g in range(1, N_GROUPS):
+        for g in range(N_GROUPS):
+            group = slice(g * OUT, (g + 1) * OUT)
+            scales_rows = repeat_on_all_partitions(g)
             nc.vector.scalar_tensor_tensor(
-                weights[:, g * OUT : (g + 1) * OUT],
-                codes[:, g * OUT : (g + 1) * OUT],
-                HALF_LOW,
-                scales_low_rows[:, (g - 1) * OUT : g * OUT],
-                SUBTRACT,
-                MULT,
+                weights[:, group], codes[:, group], HALF_HIGH if g == 0 else HALF_LOW, scales_rows[:], SUBTRACT, MULT
             )
+        bias_rows = held.tile([P, OUT], F32, name="bias_rows")
+        nc.vector.tensor_copy(bias_rows[:], repeat_on_all_partitions(N_GROUPS)[:])
 
         def look_up_and_flip(b):
             picked = work.tile([P, PICKED], F32, name="picked")
@@ -98,7 +100,7 @@ def tile_cprpackedlinear_kernel(tc, x, q_high, q_low, scales_high, scales_low, b
             return flipped
 
         def multiply_and_store(b, flipped):
-            sums = sum_banks.tile([P, OUT], F32, name="sums")
+            sums = float_banks.tile([P, OUT], F32, name="sums", tag="float_bank")
             for g in range(N_GROUPS):
                 nc.tensor.matmul(
                     sums[:],
@@ -111,8 +113,8 @@ def tile_cprpackedlinear_kernel(tc, x, q_high, q_low, scales_high, scales_low, b
             nc.vector.tensor_tensor(result[:], sums[:], bias_rows[:], ADD)
             nc.sync.dma_start(out[b * P : (b + 1) * P, :], result[:])
 
-        flipped_tiles = [look_up_and_flip(0)]
+        flipped_tiles = [look_up_and_flip(b) for b in range(BLOCKS_AHEAD)]
         for b in range(N_BLOCKS):
-            if b + 1 < N_BLOCKS:
-                flipped_tiles.append(look_up_and_flip(b + 1))
+            if b + BLOCKS_AHEAD < N_BLOCKS:
+                flipped_tiles.append(look_up_and_flip(b + BLOCKS_AHEAD))
             multiply_and_store(b, flipped_tiles[b])

@@ -35,14 +35,16 @@ def tile_cprpackedlinear_kernel(tc, x, q_high, q_low, scales_high, scales_low, b
         offsets = held.tile([P, PICKED // 16], U16, name="offsets")
         nc.sync.dma_start(offsets[:], offs)
 
+        windows = [held.tile([P, FEATURES], F32, name=f"window{b}") for b in range(N_BLOCKS)]
+        nc.sync.dma_start(windows[0][:], x[0:P, :])
+
         row_pieces = held.tile([P, P], F32, name="row_pieces")
         nc.gpsimd.memset(row_pieces[:], 0.0)
         nc.sync.dma_start(row_pieces[0:PIECES, :], scales_high.rearrange("g (k n) -> (g k) n", n=P))
         nc.sync.dma_start(row_pieces[PIECES : N_GROUPS * PIECES, :], scales_low.rearrange("g (k n) -> (g k) n", n=P))
         nc.sync.dma_start(row_pieces[N_GROUPS * PIECES : N_ROWS * PIECES, :], bias.rearrange("g (k n) -> (g k) n", n=P))
 
-        windows = [held.tile([P, FEATURES], F32, name=f"window{b}") for b in range(N_BLOCKS)]
-        for b in range(BLOCKS_BEFORE_WEIGHTS):
+        for b in range(1, BLOCKS_BEFORE_WEIGHTS):
             nc.sync.dma_start(windows[b][:], x[b * P : (b + 1) * P, :])
 
         codes = held.tile([P, N_GROUPS * OUT], BF16, name="codes")

@@ -61,13 +61,11 @@ def tile_cprpackedlinear_kernel(tc, x, q_high, q_low, scales_high, scales_low, b
         nc.vector.memset(warm_in[:], 0.0)
         nc.scalar.activation(warm_out[:], warm_in[:], COPY)
 
-        identity = held.tile([P, P], BF16, name="identity")
+        identity = held.tile([P, P], F32, name="identity")
         make_identity(nc, identity[:])
-        identity_f32 = held.tile([P, P], F32, name="identity_f32")
-        make_identity(nc, identity_f32[:])
 
         columns_bank = float_banks.tile([P, P], F32, name="columns_bank", tag="float_bank")
-        nc.tensor.transpose(columns_bank[:], row_pieces[:], identity_f32[:])
+        nc.tensor.transpose(columns_bank[:], row_pieces[:], identity[:])
         columns = held.tile([P, N_ROWS * PIECES], F32, name="columns")
         nc.vector.tensor_copy(columns[:], columns_bank[:, 0 : N_ROWS * PIECES])
 
@@ -75,7 +73,7 @@ def tile_cprpackedlinear_kernel(tc, x, q_high, q_low, scales_high, scales_low, b
             repeated = float_banks.tile([P, OUT], F32, name="repeated", tag="float_bank")
             for k in range(PIECES):
                 column = columns[:, r * PIECES + k : r * PIECES + k + 1]
-                nc.tensor.transpose(repeated[:, k * P : (k + 1) * P], column.to_broadcast([P, P]), identity_f32[:])
+                nc.tensor.transpose(repeated[:, k * P : (k + 1) * P], column.to_broadcast([P, P]), identity[:])
             return repeated
 
         weights = held.tile([P, N_GROUPS * OUT], BF16, name="weights")
@@ -91,12 +89,10 @@ def tile_cprpackedlinear_kernel(tc, x, q_high, q_low, scales_high, scales_low, b
         def look_up_and_flip(b):
             picked = work.tile([P, PICKED], F32, name="picked")
             nc.scalar.activation(picked[:], windows[b][:].indirect(offsets[:]), COPY)
-            rounded = work.tile([P, PICKED], BF16, name="rounded")
-            nc.gpsimd.tensor_copy(rounded[:], picked[:])
-            flipped_psum = flip_banks.tile([P, PICKED], BF16, name="flipped_psum")
+            flipped_psum = flip_banks.tile([P, PICKED], F32, name="flipped_psum")
             for g in range(N_GROUPS):
                 square = slice(g * GROUP, (g + 1) * GROUP)
-                nc.tensor.transpose(flipped_psum[:, square], rounded[:, square], identity[:])
+                nc.tensor.transpose(flipped_psum[:, square], picked[:, square], identity[:])
             flipped = work.tile([P, PICKED], BF16, name="flipped")
             nc.vector.tensor_copy(flipped[:], flipped_psum[:])
             return flipped

@@ -83,8 +83,6 @@ def tile_cprpackedlinear_kernel(tc, x, q_high, q_low, scales_high, scales_low, b
             nc.vector.scalar_tensor_tensor(
                 weights[:, group], codes[:, group], HALF_HIGH if g == 0 else HALF_LOW, scales_rows[:], SUBTRACT, MULT
             )
-        bias_rows = held.tile([P, OUT], F32, name="bias_rows")
-        nc.vector.tensor_copy(bias_rows[:], repeat_on_all_partitions(N_GROUPS)[:])
 
         def look_up_and_flip(b):
             picked = work.tile([P, PICKED], F32, name="picked")
@@ -112,6 +110,8 @@ def tile_cprpackedlinear_kernel(tc, x, q_high, q_low, scales_high, scales_low, b
             nc.sync.dma_start(out[b * P : (b + 1) * P, :], result[:])
 
         flipped_tiles = [look_up_and_flip(b) for b in range(BLOCKS_AHEAD)]
+        bias_rows = held.tile([P, OUT], F32, name="bias_rows")
+        nc.vector.tensor_copy(bias_rows[:], repeat_on_all_partitions(N_GROUPS)[:])
         for b in range(N_BLOCKS):
             if b + BLOCKS_AHEAD < N_BLOCKS:
                 flipped_tiles.append(look_up_and_flip(b + BLOCKS_AHEAD))

@@ -32,11 +32,11 @@ def tile_cprpackedlinear_kernel(tc, x, q_high, q_low, scales_high, scales_low, b
         tc.psum_pool(name="flip_banks", bufs=3) as flip_banks,
         tc.psum_pool(name="float_banks", bufs=N_ROWS) as float_banks,
     ):
-        offsets = held.tile([P, PICKED // 16], U16, name="offsets")
-        nc.sync.dma_start(offsets[:], offs)
-
         windows = [held.tile([P, FEATURES], F32, name=f"window{b}") for b in range(N_BLOCKS)]
         nc.sync.dma_start(windows[0][:], x[0:P, :])
+
+        offsets = held.tile([P, PICKED // 16], U16, name="offsets")
+        nc.sync.dma_start(offsets[:], offs)
 
         row_pieces = held.tile([P, P], F32, name="row_pieces")
         nc.gpsimd.memset(row_pieces[:], 0.0)
@@ -76,6 +76,52 @@ def tile_cprpackedlinear_kernel(tc, x, q_high, q_low, scales_high, scales_low, b
                 nc.tensor.transpose(repeated[:, k * P : (k + 1) * P], column.to_broadcast([P, P]), identity[:])
             return repeated
 
+        def look_up(b):
+            picked = work.tile([P, PICKED], F32, name="picked")
+            nc.scalar.activation(picked[:], windows[b][:].indirect(offsets[:]), COPY)
+            flipped_psum = flip_banks.tile([P, PICKED], F32, name="flipped_psum")
+            return picked, flipped_psum
+
+        def flip_square(picked, flipped_psum, g):
+            square = slice(g * GROUP, (g + 1) * GROUP)
+            nc.tensor.transpose(flipped_psum[:, square], picked[:, square], identity[:])
+
+        def round_flipped(flipped_psum):
+            flipped = work.tile([P, PICKED], BF16, name="flipped")
+            nc.vector.tensor_copy(flipped[:], flipped_psum[:])
+            return flipped
+
+        def look_up_and_flip(b):
+            picked, flipped_psum = look_up(b)
+            for g in range(N_GROUPS):
+                flip_square(picked, flipped_psum, g)
+            return round_flipped(flipped_psum)
+
+        def multiply_and_store(b, flipped, n_parts, block_ahead):
+            if block_ahead < N_BLOCKS:
+                picked, flipped_psum = look_up(block_ahead)
+            result = results.tile([P, OUT], F32, name="result")
+            width = OUT // n_parts
+            for i in range(n_parts):
+                sums = float_banks.tile([P, width], F32, name="sums", tag="float_bank")
+                for g in range(N_GROUPS):
+                    if block_ahead < N_BLOCKS:
+                        flip_square(picked, flipped_psum, g)
+                    nc.tensor.matmul(
+                        sums[:],
+                        flipped[:, g * GROUP : (g + 1) * GROUP],
+                        weights[:, g * OUT + i * width : g * OUT + (i + 1) * width],
+                        start=(g == 0),
+                        stop=(g == N_GROUPS - 1),
+                    )
+                if block_ahead < N_BLOCKS:
+                    flipped_tiles.append(round_flipped(flipped_psum))
+                part = slice(i * width, (i + 1) * width)
+                nc.vector.tensor_tensor(result[:, part], sums[:], bias_rows[:, part], ADD)
+            nc.sync.dma_start(out[b * P : (b + 1) * P, :], result[:])
+
+        flipped_tiles = [look_up_and_flip(0)]
+
         weights = held.tile([P, N_GROUPS * OUT], BF16, name="weights")
         for g in range(N_GROUPS):
             group = slice(g * OUT, (g + 1) * OUT)
@@ -84,35 +130,8 @@ def tile_cprpackedlinear_kernel(tc, x, q_high, q_low, scales_high, scales_low, b
                 weights[:, group], codes[:, group], HALF_HIGH if g == 0 else HALF_LOW, scales_rows[:], SUBTRACT, MULT
             )
 
-        def look_up_and_flip(b):
-            picked = work.tile([P, PICKED], F32, name="picked")
-            nc.scalar.activation(picked[:], windows[b][:].indirect(offsets[:]), COPY)
-            flipped_psum = flip_banks.tile([P, PICKED], F32, name="flipped_psum")
-            for g in range(N_GROUPS):
-                square = slice(g * GROUP, (g + 1) * GROUP)
-                nc.tensor.transpose(flipped_psum[:, square], picked[:, square], identity[:])
-            flipped = work.tile([P, PICKED], BF16, name="flipped")
-            nc.vector.tensor_copy(flipped[:], flipped_psum[:])
-            return flipped
-
-        def multiply_and_store(b, flipped):
-            sums = float_banks.tile([P, OUT], F32, name="sums", tag="float_bank")
-            for g in range(N_GROUPS):
-                nc.tensor.matmul(
-                    sums[:],
-                    flipped[:, g * GROUP : (g + 1) * GROUP],
-                    weights[:, g * OUT : (g + 1) * OUT],
-                    start=(g == 0),
-                    stop=(g == N_GROUPS - 1),
-                )
-            result = results.tile([P, OUT], F32, name="result")
-            nc.vector.tensor_tensor(result[:], sums[:], bias_rows[:], ADD)
-            nc.sync.dma_start(out[b * P : (b + 1) * P, :], result[:])
-
-        flipped_tiles = [look_up_and_flip(b) for b in range(BLOCKS_AHEAD)]
+        flipped_tiles.append(look_up_and_flip(1))
         bias_rows = held.tile([P, OUT], F32, name="bias_rows")
         nc.vector.tensor_copy(bias_rows[:], repeat_on_all_partitions(N_GROUPS)[:])
         for b in range(N_BLOCKS):
-            if b + BLOCKS_AHEAD < N_BLOCKS:
-                flipped_tiles.append(look_up_and_flip(b + BLOCKS_AHEAD))
-            multiply_and_store(b, flipped_tiles[b])
+            multiply_and_store(b, flipped_tiles[b], 2 if b == N_BLOCKS - 1 else 1, b + BLOCKS_AHEAD)

@@ -118,7 +118,7 @@ def tile_cprpackedlinear_kernel(tc, x, q_high, q_low, scales_high, scales_low, b
                     flipped_tiles.append(round_flipped(flipped_psum))
                 part = slice(i * width, (i + 1) * width)
                 nc.vector.tensor_tensor(result[:, part], sums[:], bias_rows[:, part], ADD)
-            nc.sync.dma_start(out[b * P : (b + 1) * P, :], result[:])
+                nc.sync.dma_start(out[b * P : (b + 1) * P, part], result[:, part])
 
         flipped_tiles = [look_up_and_flip(0)]
 

@@ -40,9 +40,9 @@ def tile_cprpackedlinear_kernel(tc, x, q_high, q_low, scales_high, scales_low, b
 
         row_pieces = held.tile([P, P], F32, name="row_pieces")
         nc.gpsimd.memset(row_pieces[:], 0.0)
-        nc.sync.dma_start(row_pieces[0:PIECES, :], scales_high.rearrange("g (k n) -> (g k) n", n=P))
-        nc.sync.dma_start(row_pieces[PIECES : N_GROUPS * PIECES, :], scales_low.rearrange("g (k n) -> (g k) n", n=P))
-        nc.sync.dma_start(row_pieces[N_GROUPS * PIECES : N_ROWS * PIECES, :], bias.rearrange("g (k n) -> (g k) n", n=P))
+        rows = [scales_high] + [scales_low[g : g + 1, :] for g in range(N_GROUPS - 1)] + [bias]
+        for r in range(N_ROWS):
+            nc.sync.dma_start(row_pieces[r * PIECES : (r + 1) * PIECES, :], rows[r].rearrange("g (k n) -> (g k) n", n=P))
 
         for b in range(1, BLOCKS_BEFORE_WEIGHTS):
             nc.sync.dma_start(windows[b][:], x[b * P : (b + 1) * P, :])

@@ -76,9 +76,16 @@ def tile_cprpackedlinear_kernel(tc, x, q_high, q_low, scales_high, scales_low, b
                 nc.tensor.transpose(repeated[:, k * P : (k + 1) * P], column.to_broadcast([P, P]), identity[:])
             return repeated
 
+        def halves_of(b):
+            n = 2 if b == N_BLOCKS - 1 else 1
+            return [(i * PICKED // n, (i + 1) * PICKED // n) for i in range(n)]
+
         def look_up(b):
             picked = work.tile([P, PICKED], F32, name="picked")
-            nc.scalar.activation(picked[:], windows[b][:].indirect(offsets[:]), COPY)
+            for first, end in halves_of(b):
+                nc.scalar.activation(
+                    picked[:, first:end], windows[b][:].indirect(offsets[:, first // 16 : end // 16]), COPY
+                )
             flipped_psum = flip_banks.tile([P, PICKED], F32, name="flipped_psum")
             return picked, flipped_psum
 
@@ -86,16 +93,18 @@ def tile_cprpackedlinear_kernel(tc, x, q_high, q_low, scales_high, scales_low, b
             square = slice(g * GROUP, (g + 1) * GROUP)
             nc.tensor.transpose(flipped_psum[:, square], picked[:, square], identity[:])
 
-        def round_flipped(flipped_psum):
+        def round_flipped(b, flipped_psum):
             flipped = work.tile([P, PICKED], BF16, name="flipped")
-            nc.vector.tensor_copy(flipped[:], flipped_psum[:])
+            copy = nc.scalar.copy if b == N_BLOCKS - 1 else nc.vector.tensor_copy
+            for first, end in halves_of(b):
+                copy(flipped[:, first:end], flipped_psum[:, first:end])
             return flipped
 
         def look_up_and_flip(b):
             picked, flipped_psum = look_up(b)
             for g in range(N_GROUPS):
                 flip_square(picked, flipped_psum, g)
-            return round_flipped(flipped_psum)
+            return round_flipped(b, flipped_psum)
 
         def multiply_and_store(b, flipped, n_parts, block_ahead):
             if block_ahead < N_BLOCKS:
@@ -115,7 +124,7 @@ def tile_cprpackedlinear_kernel(tc, x, q_high, q_low, scales_high, scales_low, b
                         stop=(g == N_GROUPS - 1),
                     )
                 if block_ahead < N_BLOCKS:
-                    flipped_tiles.append(round_flipped(flipped_psum))
+                    flipped_tiles.append(round_flipped(block_ahead, flipped_psum))
                 part = slice(i * width, (i + 1) * width)
                 nc.vector.tensor_tensor(result[:, part], sums[:], bias_rows[:, part], ADD)
                 nc.sync.dma_start(out[b * P : (b + 1) * P, part], result[:, part])

import concourse.mybir as mybir
from concourse.masks import make_identity

F32, BF16, U16 = mybir.dt.float32, mybir.dt.bfloat16, mybir.dt.uint16
COPY = mybir.ActivationFunctionType.Copy
ADD, SUBTRACT, MULT = mybir.AluOpType.add, mybir.AluOpType.subtract, mybir.AluOpType.mult

P = 128
TOKENS = 1024
FEATURES = 1024
PICKED = 512
OUT = 512
GROUP = 128
N_GROUPS = PICKED // GROUP
N_BLOCKS = TOKENS // P
HALF_HIGH, HALF_LOW = 31.0, 15.0

FLOPS = 2 * TOKENS * PICKED * OUT

N_ROWS = N_GROUPS + 1
PIECES = OUT // P
BLOCKS_AHEAD = 2
BLOCKS_BEFORE_WEIGHTS = 2


def tile_cprpackedlinear_kernel(tc, x, q_high, q_low, scales_high, scales_low, bias, offs, out):
    nc = tc.nc
    with (
        tc.tile_pool(name="held", bufs=1) as held,
        tc.tile_pool(name="work", bufs=4) as work,
        tc.tile_pool(name="results", bufs=N_BLOCKS) as results,
        tc.psum_pool(name="flip_banks", bufs=3) as flip_banks,
        tc.psum_pool(name="float_banks", bufs=N_ROWS) as float_banks,
    ):
        windows = [held.tile([P, FEATURES], F32, name=f"window{b}") for b in range(N_BLOCKS)]
        nc.sync.dma_start(windows[0][:], x[0:P, :])

        offsets = held.tile([P, PICKED // 16], U16, name="offsets")
        nc.sync.dma_start(offsets[:], offs)

        row_pieces = held.tile([P, P], F32, name="row_pieces")
        nc.gpsimd.memset(row_pieces[:], 0.0)
        rows = [scales_high] + [scales_low[g : g + 1, :] for g in range(N_GROUPS - 1)] + [bias]
        for r in range(N_ROWS):
            nc.sync.dma_start(row_pieces[r * PIECES : (r + 1) * PIECES, :], rows[r].rearrange("g (k n) -> (g k) n", n=P))

        for b in range(1, BLOCKS_BEFORE_WEIGHTS):
            nc.sync.dma_start(windows[b][:], x[b * P : (b + 1) * P, :])

        codes = held.tile([P, N_GROUPS * OUT], BF16, name="codes")
        nc.sync.dma_start(codes[:, 0:OUT], q_high)
        nc.sync.dma_start(
            codes[:, OUT:].rearrange("p (g o) -> p g o", o=OUT), q_low.rearrange("(g p) o -> p g o", p=P)
        )

        for b in range(BLOCKS_BEFORE_WEIGHTS, N_BLOCKS):
            nc.sync.dma_start(windows[b][:], x[b * P : (b + 1) * P, :])

        warm_in = held.tile([P, 1], F32, name="warm_in")
        warm_out = held.tile([P, 1], F32, name="warm_out")
        nc.vector.memset(warm_in[:], 0.0)
        nc.scalar.activation(warm_out[:], warm_in[:], COPY)

        identity = held.tile([P, P], F32, name="identity")
        make_identity(nc, identity[:])

        columns_bank = float_banks.tile([P, P], F32, name="columns_bank", tag="float_bank")
        nc.tensor.transpose(columns_bank[:], row_pieces[:], identity[:])
        columns = held.tile([P, N_ROWS * PIECES], F32, name="columns")
        nc.vector.tensor_copy(columns[:], columns_bank[:, 0 : N_ROWS * PIECES])

        def repeat_on_all_partitions(r):
            repeated = float_banks.tile([P, OUT], F32, name="repeated", tag="float_bank")
            for k in range(PIECES):
                column = columns[:, r * PIECES + k : r * PIECES + k + 1]
                nc.tensor.transpose(repeated[:, k * P : (k + 1) * P], column.to_broadcast([P, P]), identity[:])
            return repeated

        def halves_of(b):
            n = 2 if b == N_BLOCKS - 1 else 1
            return [(i * PICKED // n, (i + 1) * PICKED // n) for i in range(n)]

        def look_up(b):
            picked = work.tile([P, PICKED], F32, name="picked")
            for first, end in halves_of(b):
                nc.scalar.activation(
                    picked[:, first:end], windows[b][:].indirect(offsets[:, first // 16 : end // 16]), COPY
                )
            flipped_psum = flip_banks.tile([P, PICKED], F32, name="flipped_psum")
            return picked, flipped_psum

        def flip_square(picked, flipped_psum, g):
            square = slice(g * GROUP, (g + 1) * GROUP)
            nc.tensor.transpose(flipped_psum[:, square], picked[:, square], identity[:])

        def round_flipped(b, flipped_psum):
            flipped = work.tile([P, PICKED], BF16, name="flipped")
            copy = nc.scalar.copy if b == N_BLOCKS - 1 else nc.vector.tensor_copy
            for first, end in halves_of(b):
                copy(flipped[:, first:end], flipped_psum[:, first:end])
            return flipped

        def look_up_and_flip(b):
            picked, flipped_psum = look_up(b)
            for g in range(N_GROUPS):
                flip_square(picked, flipped_psum, g)
            return round_flipped(b, flipped_psum)

        def multiply_and_store(b, flipped, n_parts, block_ahead):
            if block_ahead < N_BLOCKS:
                picked, flipped_psum = look_up(block_ahead)
            result = results.tile([P, OUT], F32, name="result")
            width = OUT // n_parts
            for i in range(n_parts):
                sums = float_banks.tile([P, width], F32, name="sums", tag="float_bank")
                for g in range(N_GROUPS):
                    if block_ahead < N_BLOCKS:
                        flip_square(picked, flipped_psum, g)
                    nc.tensor.matmul(
                        sums[:],
                        flipped[:, g * GROUP : (g + 1) * GROUP],
                        weights[:, g * OUT + i * width : g * OUT + (i + 1) * width],
                        start=(g == 0),
                        stop=(g == N_GROUPS - 1),
                    )
                if block_ahead < N_BLOCKS:
                    flipped_tiles.append(round_flipped(block_ahead, flipped_psum))
                part = slice(i * width, (i + 1) * width)
                nc.vector.tensor_tensor(result[:, part], sums[:], bias_rows[:, part], ADD)
                nc.sync.dma_start(out[b * P : (b + 1) * P, part], result[:, part])

        flipped_tiles = [look_up_and_flip(0)]

        weights = held.tile([P, N_GROUPS * OUT], BF16, name="weights")
        for g in range(N_GROUPS):
            group = slice(g * OUT, (g + 1) * OUT)
            scales_rows = repeat_on_all_partitions(g)
            nc.vector.scalar_tensor_tensor(
                weights[:, group], codes[:, group], HALF_HIGH if g == 0 else HALF_LOW, scales_rows[:], SUBTRACT, MULT
            )

        flipped_tiles.append(look_up_and_flip(1))
        bias_rows = held.tile([P, OUT], F32, name="bias_rows")
        nc.vector.tensor_copy(bias_rows[:], repeat_on_all_partitions(N_GROUPS)[:])
        for b in range(N_BLOCKS):
            multiply_and_store(b, flipped_tiles[b], 2 if b == N_BLOCKS - 1 else 1, b + BLOCKS_AHEAD)
